import numpy as np
import ml_dtypes


def mxq(x, axis, fmt="e4m3"):
    dtype, down = {"e4m3": (ml_dtypes.float8_e4m3fn, 7), "e5m2": (ml_dtypes.float8_e5m2, 14)}[fmt]
    v = np.moveaxis(np.asarray(x, np.float32).astype(ml_dtypes.bfloat16).astype(np.float64), axis, -1)
    blocks = v.reshape(v.shape[:-1] + (-1, 32))
    amax = np.abs(blocks).max(-1, keepdims=True)
    byte = np.maximum(np.where(amax > 0, np.frexp(amax)[1] - 1 + 127, 0) - down, 1)
    scale = np.exp2(byte - 127.0)
    codes = (blocks / scale).astype(np.float32).astype(dtype).astype(np.float64)
    return np.moveaxis((codes * scale).reshape(v.shape), -1, axis)


WIDE = False


def mx_kscale(k):
    if not WIDE:
        return np.ones(k)
    levels = np.array([10, -10, 5, -5, 0])
    a = np.random.permutation(np.resize(levels, k // 512 * 4)).reshape(k // 512, 4)
    idx = np.arange(k)
    return np.exp2(a[idx // 512, idx % 128 // 32])


BF16 = ml_dtypes.bfloat16


def bf(x):
    return np.asarray(x, np.float32).astype(BF16)


def f64(x):
    return np.asarray(x).astype(np.float64)


B, T, D, H, KV, DH = 4, 2048, 1024, 2, 1, 32
G = H // KV
HALF = DH // 2
ROPE_THETA = 1e6
YARN_FACTOR = 64.0
ORIG_MAX_POS = 4096.0
BETA_FAST, BETA_SLOW = 4.0, 1.0
ATTN_FACTOR = 0.1 * np.log(YARN_FACTOR) + 1.0


def corr_dim(num_rot):
    return DH * np.log(ORIG_MAX_POS / (num_rot * 2 * np.pi)) / (2 * np.log(ROPE_THETA))


def yarn_inv_freq():
    low = float(np.sum(np.arange(DH) + 1 <= corr_dim(BETA_FAST)))
    high = min(float(np.sum(np.arange(DH) < corr_dim(BETA_SLOW))), DH - 1.0)
    if low == high:
        high += 0.001
    ramp = np.clip((np.arange(HALF) - low) / (high - low), 0.0, 1.0)
    pos_freqs = ROPE_THETA ** (np.arange(0, DH, 2) / DH)
    inv_extrap = 1.0 / pos_freqs
    inv_interp = 1.0 / (YARN_FACTOR * pos_freqs)
    extrap_factor = 1.0 - ramp
    return inv_interp * (1.0 - extrap_factor) + inv_extrap * extrap_factor


def rope_yarn(v):
    angles = np.arange(T)[:, None] * yarn_inv_freq()[None, :]
    cos = np.cos(angles)[None, :, None, :]
    sin = np.sin(angles)[None, :, None, :]
    v_even = v[..., 0::2]
    v_odd = v[..., 1::2]
    out_even = v_even * cos - v_odd * sin
    out_odd = v_even * sin + v_odd * cos
    return np.stack([out_even, out_odd], axis=-1).reshape(v.shape) * ATTN_FACTOR


def setup_inputs():
    s = mx_kscale(D)
    return {"x": bf(np.random.standard_normal((B, T, D)) * s),
            "w_qkv": bf(np.random.standard_normal((D, (H + 2 * KV) * DH)) / np.sqrt(D) / s[:, None])}


def reference(x, w_qkv):
    qkv = mxq(f64(x), 2, "e4m3") @ mxq(f64(w_qkv), 0, "e4m3")
    q = qkv[:, :, :H * DH].reshape(B, T, H, DH)
    k = qkv[:, :, H * DH:(H + KV) * DH].reshape(B, T, KV, DH)
    v = qkv[:, :, (H + KV) * DH:].reshape(B, T, KV, DH)
    q = rope_yarn(q)
    k = rope_yarn(k)
    q = q.reshape(B, T, KV, G, DH).transpose(0, 2, 3, 1, 4)
    k = k.transpose(0, 2, 1, 3)
    v = v.transpose(0, 2, 1, 3)
    return q, k, v

@@ -1,0 +1,258 @@
+import math
+from contextlib import ExitStack
+
+import concourse.mybir as mybir
+from concourse.masks import make_identity
+
+F32 = mybir.dt.float32
+BF16 = mybir.dt.bfloat16
+I32 = mybir.dt.int32
+U32 = mybir.dt.uint32
+U8 = mybir.dt.uint8
+FP8X4 = mybir.dt.float8_e4m3fn_x4
+ALU = mybir.AluOpType
+ACT = mybir.ActivationFunctionType
+
+P = 128
+BATCH = 4
+SEQ = 2048
+D_MODEL = 1024
+HEAD_DIM = 32
+PAIRS = HEAD_DIM // 2
+ROPE_HEADS = 3
+HEADS = 4
+FEATURES = HEADS * HEAD_DIM
+
+PACK = 4
+K_PASS = P * PACK
+PASSES = D_MODEL // K_PASS
+WORD_BLOCKS = 2
+
+TILES = SEQ // P
+CHUNK_TILES = 4
+CHUNKS = TILES // CHUNK_TILES
+QUANT_TILES = 2
+STORE_CHUNKS = 2
+STORE_TILES = STORE_CHUNKS * CHUNK_TILES
+
+ROPE_THETA = 1e6
+YARN_FACTOR = 64.0
+RAMP_LOW = 5.0
+RAMP_HIGH = 8.0
+ATTN_FACTOR = 0.1 * math.log(YARN_FACTOR) + 1.0
+TURN_GRID = 2.0**15
+ROUND_MAGIC = 1.5 * 2.0**23
+
+FLOPS = 2 * BATCH * SEQ * D_MODEL * FEATURES
+
+
+def turns_per_position(i):
+    base = ROPE_THETA ** (-i / PAIRS)
+    ramp = min(max((i - RAMP_LOW) / (RAMP_HIGH - RAMP_LOW), 0.0), 1.0)
+    return (base * (1.0 - ramp) + (base / YARN_FACTOR) * ramp) / (2.0 * math.pi)
+
+
+def build_rope_tables(nc, pool, cos_tab, sin_tab):
+    both = [P, 2, TILES, PAIRS]
+    pos_int = pool.tile([P, TILES], I32)
+    nc.gpsimd.iota(pos_int[:], pattern=[[1, TILES]], base=0, channel_multiplier=TILES)
+    pos = pool.tile([P, TILES], F32)
+    nc.vector.tensor_copy(out=pos[:], in_=pos_int[:])
+
+    coarse = pool.tile(both, F32)
+    fine = pool.tile([P, TILES, PAIRS], F32)
+    for i in range(PAIRS):
+        turns = turns_per_position(i)
+        turns_coarse = round(turns * TURN_GRID) / TURN_GRID
+        nc.vector.tensor_scalar(
+            out=coarse[:, 0, :, i], in0=pos[:], scalar1=turns_coarse, scalar2=None, op0=ALU.mult
+        )
+        nc.vector.tensor_scalar(
+            out=fine[:, :, i], in0=pos[:], scalar1=turns - turns_coarse, scalar2=None, op0=ALU.mult
+        )
+    nc.vector.tensor_scalar(
+        out=coarse[:, 1], in0=coarse[:, 0], scalar1=-0.25, scalar2=None, op0=ALU.add
+    )
+
+    whole = pool.tile(both, F32)
+    nc.vector.tensor_scalar(
+        out=whole[:],
+        in0=coarse[:],
+        scalar1=ROUND_MAGIC,
+        scalar2=ROUND_MAGIC,
+        op0=ALU.add,
+        op1=ALU.subtract,
+    )
+    near = pool.tile(both, F32)
+    nc.vector.tensor_tensor(out=near[:], in0=coarse[:], in1=whole[:], op=ALU.subtract)
+    frac = pool.tile(both, F32)
+    nc.vector.tensor_tensor(
+        out=frac[:], in0=near[:], in1=fine[:].unsqueeze(1).to_broadcast(both), op=ALU.add
+    )
+
+    half_sin = pool.tile(both, F32)
+    nc.scalar.activation(out=half_sin[:], in_=frac[:], func=ACT.Sin, scale=math.pi)
+    versine = pool.tile(both, F32)
+    nc.scalar.activation(
+        out=versine[:], in_=half_sin[:], func=ACT.Square, scale=math.sqrt(2.0 * ATTN_FACTOR)
+    )
+
+    nc.vector.tensor_scalar(
+        out=cos_tab[:],
+        in0=versine[:, 0].unsqueeze(3).to_broadcast([P, TILES, PAIRS, 2]),
+        scalar1=-1.0,
+        scalar2=ATTN_FACTOR,
+        op0=ALU.mult,
+        op1=ALU.add,
+    )
+    nc.vector.tensor_scalar(
+        out=sin_tab[:, 0], in0=versine[:, 1], scalar1=ATTN_FACTOR, scalar2=None, op0=ALU.subtract
+    )
+    nc.vector.tensor_scalar(
+        out=sin_tab[:, 1],
+        in0=versine[:, 1],
+        scalar1=-1.0,
+        scalar2=ATTN_FACTOR,
+        op0=ALU.mult,
+        op1=ALU.add,
+    )
+
+
+def tile_causalselfattentiongqa_pa_t_kernel(tc, x, w_qkv, out_0, out_1, out_2):
+    nc = tc.nc
+    with ExitStack() as ctx:
+        const = ctx.enter_context(tc.tile_pool(name="const", bufs=1))
+        x_pool = ctx.enter_context(tc.tile_pool(name="x", bufs=8))
+        mx_pool = ctx.enter_context(tc.tile_pool(name="mx", bufs=3))
+        rope_pool = ctx.enter_context(tc.tile_pool(name="rope", bufs=3))
+        out_pool = ctx.enter_context(tc.tile_pool(name="out", bufs=3))
+        psum_t = ctx.enter_context(tc.psum_pool(name="psum_t", bufs=6))
+        psum_u = ctx.enter_context(tc.psum_pool(name="psum_u", bufs=2))
+
+        identity = const.tile([P, P], F32)
+        make_identity(nc, identity[:])
+
+        x_rows = x.rearrange("b (p j) d -> b p (j d)", j=TILES)
+
+        def load_chunk(b, c):
+            x_chunk = x_pool.tile([P, CHUNK_TILES * D_MODEL], BF16)
+            first = c * CHUNK_TILES * D_MODEL
+            nc.sync.dma_start(out=x_chunk[:], in_=x_rows[b, :, first : first + CHUNK_TILES * D_MODEL])
+            return x_chunk
+
+        first_chunk = load_chunk(0, 0)
+
+        cos_tab = const.tile([P, TILES, PAIRS, 2], F32)
+        sin_tab = const.tile([P, 2, TILES, PAIRS], F32)
+        build_rope_tables(nc, const, cos_tab, sin_tab)
+
+        w_raw = const.tile([P, PASSES, PACK, FEATURES], BF16)
+        nc.sync.dma_start(
+            out=w_raw[:].rearrange("p g (u e) c -> p (g u) (e c)", e=2),
+            in_=w_qkv.rearrange("(gu p e) c -> p gu (e c)", p=P, e=2),
+        )
+        w_grouped = const.tile([P, PASSES, FEATURES, PACK], BF16, align_bytes=64)
+        nc.vector.tensor_copy(out=w_grouped[:], in_=w_raw[:].rearrange("p g t c -> p g c t"))
+        w_codes = const.tile([P, PASSES * FEATURES], U32, align_bytes=64)
+        w_scales = const.tile([P, PASSES * FEATURES], U8, align_bytes=64)
+        nc.vector.quantize_mx(
+            out=w_codes[:].bitcast(FP8X4),
+            scales=w_scales[:],
+            in_=w_grouped[:].rearrange("p g c t -> p (g c t)"),
+        )
+
+        for b in range(BATCH):
+            for c in range(CHUNKS):
+                x_chunk = first_chunk if (b == 0 and c == 0) else load_chunk(b, c)
+                x_words = x_chunk[:].bitcast(F32)
+
+                grouped = mx_pool.tile([P, CHUNK_TILES * PASSES * P * PACK], BF16, align_bytes=64)
+                grouped_words = grouped[:].bitcast(F32).rearrange(
+                    "p (j g c u) -> p j g c u", j=CHUNK_TILES, g=PASSES, u=WORD_BLOCKS
+                )
+                codes = mx_pool.tile([P, CHUNK_TILES * PASSES * P], U32, align_bytes=64)
+                scales = mx_pool.tile([P, CHUNK_TILES * PASSES * P], U8, align_bytes=64)
+                for jj in range(CHUNK_TILES):
+                    xt = psum_t.tile([P, PASSES, WORD_BLOCKS, P], F32)
+                    for g in range(PASSES):
+                        for u in range(WORD_BLOCKS):
+                            col = ((jj * PASSES + g) * WORD_BLOCKS + u) * P
+                            nc.tensor.transpose(xt[:, g, u, :], x_words[:, col : col + P], identity[:])
+                    nc.scalar.copy(out=grouped_words[:, jj], in_=xt[:].rearrange("p g u c -> p g c u"))
+                    if jj % QUANT_TILES == QUANT_TILES - 1:
+                        words = QUANT_TILES * PASSES * P
+                        lo = (jj + 1 - QUANT_TILES) * PASSES * P
+                        nc.vector.quantize_mx(
+                            out=codes[:, lo : lo + words].bitcast(FP8X4),
+                            scales=scales[:, lo : lo + words],
+                            in_=grouped[:, lo * PACK : (lo + words) * PACK],
+                        )
+
+                u_bank = psum_u.tile([P, CHUNK_TILES, FEATURES], F32)
+                for jj in range(CHUNK_TILES):
+                    for g in range(PASSES):
+                        lo = (jj * PASSES + g) * P
+                        nc.tensor.matmul_mx(
+                            out=u_bank[:, jj, :],
+                            lhsT=codes[:, lo : lo + P].bitcast(FP8X4),
+                            lhsT_scale=scales[:, lo : lo + P],
+                            rhs=w_codes[:, g * FEATURES : (g + 1) * FEATURES].bitcast(FP8X4),
+                            rhs_scale=w_scales[:, g * FEATURES : (g + 1) * FEATURES],
+                            start=(g == 0),
+                            stop=(g == PASSES - 1),
+                        )
+
+                if c % STORE_CHUNKS == 0:
+                    out_sb = out_pool.tile([P, HEADS, STORE_TILES, HEAD_DIM], F32)
+                j_batch = c * CHUNK_TILES
+                j_store = (c % STORE_CHUNKS) * CHUNK_TILES
+
+                nc.scalar.copy(
+                    out=out_sb[:, ROPE_HEADS, j_store : j_store + CHUNK_TILES, :],
+                    in_=u_bank[:, :, ROPE_HEADS * HEAD_DIM :],
+                )
+                roped = u_bank[:, :, : ROPE_HEADS * HEAD_DIM]
+                by_cos = rope_pool.tile([P, ROPE_HEADS, CHUNK_TILES, HEAD_DIM], F32)
+                nc.vector.tensor_tensor(
+                    out=by_cos[:],
+                    in0=roped.rearrange("p j (h d) -> p h j d", h=ROPE_HEADS),
+                    in1=cos_tab[:, j_batch : j_batch + CHUNK_TILES]
+                    .rearrange("p j i two -> p j (i two)")
+                    .unsqueeze(1)
+                    .to_broadcast([P, ROPE_HEADS, CHUNK_TILES, HEAD_DIM]),
+                    op=ALU.mult,
+                )
+                by_sin = rope_pool.tile([P, 2, ROPE_HEADS, CHUNK_TILES, PAIRS], F32)
+                halves = roped.rearrange("p j (h i two) -> p two h j i", h=ROPE_HEADS, two=2)
+                for two in range(2):
+                    nc.vector.tensor_tensor(
+                        out=by_sin[:, two],
+                        in0=halves[:, 1 - two],
+                        in1=sin_tab[:, two, j_batch : j_batch + CHUNK_TILES, :]
+                        .unsqueeze(1)
+                        .to_broadcast([P, ROPE_HEADS, CHUNK_TILES, PAIRS]),
+                        op=ALU.mult,
+                    )
+                nc.vector.tensor_tensor(
+                    out=out_sb[:, :ROPE_HEADS, j_store : j_store + CHUNK_TILES, :].rearrange(
+                        "p h j (i two) -> p h j i two", two=2
+                    ),
+                    in0=by_cos[:].rearrange("p h j (i two) -> p h j i two", two=2),
+                    in1=by_sin[:].rearrange("p two h j i -> p h j i two"),
+                    op=ALU.add,
+                )
+
+                if c % STORE_CHUNKS == STORE_CHUNKS - 1:
+                    j0 = j_batch + CHUNK_TILES - STORE_TILES
+                    nc.sync.dma_start(
+                        out=out_0[b, 0].rearrange("h (p j) d -> p h j d", j=TILES)[:, :, j0 : j0 + STORE_TILES, :],
+                        in_=out_sb[:, 0:2],
+                    )
+                    nc.sync.dma_start(
+                        out=out_1[b, 0].rearrange("(p j) d -> p j d", j=TILES)[:, j0 : j0 + STORE_TILES, :],
+                        in_=out_sb[:, 2],
+                    )
+                    nc.sync.dma_start(
+                        out=out_2[b, 0].rearrange("(p j) d -> p j d", j=TILES)[:, j0 : j0 + STORE_TILES, :],
+                        in_=out_sb[:, 3],
+                    )

@@ -34,6 +34,8 @@ CHUNKS = TILES // CHUNK_TILES
 QUANT_TILES = 2
 STORE_CHUNKS = 2
 STORE_TILES = STORE_CHUNKS * CHUNK_TILES
+ALL_CHUNKS = BATCH * CHUNKS
+X_BUFS = 8
 
 ROPE_THETA = 1e6
 YARN_FACTOR = 64.0
@@ -122,35 +124,152 @@ def tile_causalselfattentiongqa_pa_t_kernel(tc, x, w_qkv, out_0, out_1, out_2):
     nc = tc.nc
     with ExitStack() as ctx:
         const = ctx.enter_context(tc.tile_pool(name="const", bufs=1))
-        x_pool = ctx.enter_context(tc.tile_pool(name="x", bufs=8))
+        x_pool = ctx.enter_context(tc.tile_pool(name="x", bufs=X_BUFS))
         mx_pool = ctx.enter_context(tc.tile_pool(name="mx", bufs=3))
         rope_pool = ctx.enter_context(tc.tile_pool(name="rope", bufs=3))
         out_pool = ctx.enter_context(tc.tile_pool(name="out", bufs=3))
         psum_t = ctx.enter_context(tc.psum_pool(name="psum_t", bufs=6))
         psum_u = ctx.enter_context(tc.psum_pool(name="psum_u", bufs=2))
-
-        identity = const.tile([P, P], F32)
-        make_identity(nc, identity[:])
+        ctx.enter_context(tc.manual_schedule())
 
         x_rows = x.rearrange("b (p j) d -> b p (j d)", j=TILES)
+        x_chunks = {}
+        mx_tiles = {}
+        u_banks = {}
+        rope_tiles = {}
+        out_tiles = {}
 
-        def load_chunk(b, c):
+        def load(n):
+            b, c = divmod(n, CHUNKS)
             x_chunk = x_pool.tile([P, CHUNK_TILES * D_MODEL], BF16)
             first = c * CHUNK_TILES * D_MODEL
             nc.sync.dma_start(out=x_chunk[:], in_=x_rows[b, :, first : first + CHUNK_TILES * D_MODEL])
-            return x_chunk
+            x_chunks[n] = x_chunk
 
-        first_chunk = load_chunk(0, 0)
+        def transpose_and_quantise(n, half):
+            if half == 0:
+                grouped = mx_pool.tile([P, CHUNK_TILES * PASSES * P * PACK], BF16, align_bytes=64)
+                codes = mx_pool.tile([P, CHUNK_TILES * PASSES * P], U32, align_bytes=64)
+                scales = mx_pool.tile([P, CHUNK_TILES * PASSES * P], U8, align_bytes=64)
+                mx_tiles[n] = (grouped, codes, scales)
+            grouped, codes, scales = mx_tiles[n]
+            x_words = x_chunks[n][:].bitcast(F32)
+            grouped_words = grouped[:].bitcast(F32).rearrange(
+                "p (j g c u) -> p j g c u", j=CHUNK_TILES, g=PASSES, u=WORD_BLOCKS
+            )
+            for jj in range(half * QUANT_TILES, (half + 1) * QUANT_TILES):
+                xt = psum_t.tile([P, PASSES, WORD_BLOCKS, P], F32)
+                for g in range(PASSES):
+                    for u in range(WORD_BLOCKS):
+                        col = ((jj * PASSES + g) * WORD_BLOCKS + u) * P
+                        nc.tensor.transpose(xt[:, g, u, :], x_words[:, col : col + P], identity[:])
+                nc.scalar.copy(out=grouped_words[:, jj], in_=xt[:].rearrange("p g u c -> p g c u"))
+            words = QUANT_TILES * PASSES * P
+            lo = half * words
+            nc.vector.quantize_mx(
+                out=codes[:, lo : lo + words].bitcast(FP8X4),
+                scales=scales[:, lo : lo + words],
+                in_=grouped[:, lo * PACK : (lo + words) * PACK],
+            )
 
-        cos_tab = const.tile([P, TILES, PAIRS, 2], F32)
-        sin_tab = const.tile([P, 2, TILES, PAIRS], F32)
-        build_rope_tables(nc, const, cos_tab, sin_tab)
+        def project(n):
+            grouped, codes, scales = mx_tiles[n]
+            u_bank = psum_u.tile([P, CHUNK_TILES, FEATURES], F32)
+            for jj in range(CHUNK_TILES):
+                for g in range(PASSES):
+                    lo = (jj * PASSES + g) * P
+                    nc.tensor.matmul_mx(
+                        out=u_bank[:, jj, :],
+                        lhsT=codes[:, lo : lo + P].bitcast(FP8X4),
+                        lhsT_scale=scales[:, lo : lo + P],
+                        rhs=w_codes[:, g * FEATURES : (g + 1) * FEATURES].bitcast(FP8X4),
+                        rhs_scale=w_scales[:, g * FEATURES : (g + 1) * FEATURES],
+                        start=(g == 0),
+                        stop=(g == PASSES - 1),
+                    )
+            u_banks[n] = u_bank
 
+        def rope_products(n):
+            c = n % CHUNKS
+            if c % STORE_CHUNKS == 0:
+                out_sb = out_pool.tile([P, HEADS, STORE_TILES, HEAD_DIM], F32)
+                out_tiles[n // STORE_CHUNKS] = out_sb
+            out_sb = out_tiles[n // STORE_CHUNKS]
+            u_bank = u_banks[n]
+            j_batch = c * CHUNK_TILES
+            j_store = (c % STORE_CHUNKS) * CHUNK_TILES
+            nc.scalar.copy(
+                out=out_sb[:, ROPE_HEADS, j_store : j_store + CHUNK_TILES, :],
+                in_=u_bank[:, :, ROPE_HEADS * HEAD_DIM :],
+            )
+            roped = u_bank[:, :, : ROPE_HEADS * HEAD_DIM]
+            by_cos = rope_pool.tile([P, ROPE_HEADS, CHUNK_TILES, HEAD_DIM], F32)
+            nc.vector.tensor_tensor(
+                out=by_cos[:],
+                in0=roped.rearrange("p j (h d) -> p h j d", h=ROPE_HEADS),
+                in1=cos_tab[:, j_batch : j_batch + CHUNK_TILES]
+                .rearrange("p j i two -> p j (i two)")
+                .unsqueeze(1)
+                .to_broadcast([P, ROPE_HEADS, CHUNK_TILES, HEAD_DIM]),
+                op=ALU.mult,
+            )
+            by_sin = rope_pool.tile([P, 2, ROPE_HEADS, CHUNK_TILES, PAIRS], F32)
+            halves = roped.rearrange("p j (h i two) -> p two h j i", h=ROPE_HEADS, two=2)
+            for two in range(2):
+                nc.vector.tensor_tensor(
+                    out=by_sin[:, two],
+                    in0=halves[:, 1 - two],
+                    in1=sin_tab[:, two, j_batch : j_batch + CHUNK_TILES, :]
+                    .unsqueeze(1)
+                    .to_broadcast([P, ROPE_HEADS, CHUNK_TILES, PAIRS]),
+                    op=ALU.mult,
+                )
+            rope_tiles[n] = (by_cos, by_sin)
+
+        def rope_sum_and_store(n):
+            b, c = divmod(n, CHUNKS)
+            out_sb = out_tiles[n // STORE_CHUNKS]
+            by_cos, by_sin = rope_tiles[n]
+            j_store = (c % STORE_CHUNKS) * CHUNK_TILES
+            nc.vector.tensor_tensor(
+                out=out_sb[:, :ROPE_HEADS, j_store : j_store + CHUNK_TILES, :].rearrange(
+                    "p h j (i two) -> p h j i two", two=2
+                ),
+                in0=by_cos[:].rearrange("p h j (i two) -> p h j i two", two=2),
+                in1=by_sin[:].rearrange("p two h j i -> p h j i two"),
+                op=ALU.add,
+            )
+            if c % STORE_CHUNKS == STORE_CHUNKS - 1:
+                j0 = (c + 1) * CHUNK_TILES - STORE_TILES
+                nc.sync.dma_start(
+                    out=out_0[b, 0].rearrange("h (p j) d -> p h j d", j=TILES)[:, :, j0 : j0 + STORE_TILES, :],
+                    in_=out_sb[:, 0:2],
+                )
+                nc.sync.dma_start(
+                    out=out_1[b, 0].rearrange("(p j) d -> p j d", j=TILES)[:, j0 : j0 + STORE_TILES, :],
+                    in_=out_sb[:, 2],
+                )
+                nc.sync.dma_start(
+                    out=out_2[b, 0].rearrange("(p j) d -> p j d", j=TILES)[:, j0 : j0 + STORE_TILES, :],
+                    in_=out_sb[:, 3],
+                )
+
+        load(0)
         w_raw = const.tile([P, PASSES, PACK, FEATURES], BF16)
         nc.sync.dma_start(
             out=w_raw[:].rearrange("p g (u e) c -> p (g u) (e c)", e=2),
             in_=w_qkv.rearrange("(gu p e) c -> p gu (e c)", p=P, e=2),
         )
+        for n in range(1, X_BUFS - 1):
+            load(n)
+
+        cos_tab = const.tile([P, TILES, PAIRS, 2], F32)
+        sin_tab = const.tile([P, 2, TILES, PAIRS], F32)
+        build_rope_tables(nc, const, cos_tab, sin_tab)
+
+        identity = const.tile([P, P], F32)
+        make_identity(nc, identity[:])
+
         w_grouped = const.tile([P, PASSES, FEATURES, PACK], BF16, align_bytes=64)
         nc.vector.tensor_copy(out=w_grouped[:], in_=w_raw[:].rearrange("p g t c -> p g c t"))
         w_codes = const.tile([P, PASSES * FEATURES], U32, align_bytes=64)
@@ -161,98 +280,15 @@ def tile_causalselfattentiongqa_pa_t_kernel(tc, x, w_qkv, out_0, out_1, out_2):
             in_=w_grouped[:].rearrange("p g c t -> p (g c t)"),
         )
 
-        for b in range(BATCH):
-            for c in range(CHUNKS):
-                x_chunk = first_chunk if (b == 0 and c == 0) else load_chunk(b, c)
-                x_words = x_chunk[:].bitcast(F32)
-
-                grouped = mx_pool.tile([P, CHUNK_TILES * PASSES * P * PACK], BF16, align_bytes=64)
-                grouped_words = grouped[:].bitcast(F32).rearrange(
-                    "p (j g c u) -> p j g c u", j=CHUNK_TILES, g=PASSES, u=WORD_BLOCKS
-                )
-                codes = mx_pool.tile([P, CHUNK_TILES * PASSES * P], U32, align_bytes=64)
-                scales = mx_pool.tile([P, CHUNK_TILES * PASSES * P], U8, align_bytes=64)
-                for jj in range(CHUNK_TILES):
-                    xt = psum_t.tile([P, PASSES, WORD_BLOCKS, P], F32)
-                    for g in range(PASSES):
-                        for u in range(WORD_BLOCKS):
-                            col = ((jj * PASSES + g) * WORD_BLOCKS + u) * P
-                            nc.tensor.transpose(xt[:, g, u, :], x_words[:, col : col + P], identity[:])
-                    nc.scalar.copy(out=grouped_words[:, jj], in_=xt[:].rearrange("p g u c -> p g c u"))
-                    if jj % QUANT_TILES == QUANT_TILES - 1:
-                        words = QUANT_TILES * PASSES * P
-                        lo = (jj + 1 - QUANT_TILES) * PASSES * P
-                        nc.vector.quantize_mx(
-                            out=codes[:, lo : lo + words].bitcast(FP8X4),
-                            scales=scales[:, lo : lo + words],
-                            in_=grouped[:, lo * PACK : (lo + words) * PACK],
-                        )
-
-                u_bank = psum_u.tile([P, CHUNK_TILES, FEATURES], F32)
-                for jj in range(CHUNK_TILES):
-                    for g in range(PASSES):
-                        lo = (jj * PASSES + g) * P
-                        nc.tensor.matmul_mx(
-                            out=u_bank[:, jj, :],
-                            lhsT=codes[:, lo : lo + P].bitcast(FP8X4),
-                            lhsT_scale=scales[:, lo : lo + P],
-                            rhs=w_codes[:, g * FEATURES : (g + 1) * FEATURES].bitcast(FP8X4),
-                            rhs_scale=w_scales[:, g * FEATURES : (g + 1) * FEATURES],
-                            start=(g == 0),
-                            stop=(g == PASSES - 1),
-                        )
-
-                if c % STORE_CHUNKS == 0:
-                    out_sb = out_pool.tile([P, HEADS, STORE_TILES, HEAD_DIM], F32)
-                j_batch = c * CHUNK_TILES
-                j_store = (c % STORE_CHUNKS) * CHUNK_TILES
-
-                nc.scalar.copy(
-                    out=out_sb[:, ROPE_HEADS, j_store : j_store + CHUNK_TILES, :],
-                    in_=u_bank[:, :, ROPE_HEADS * HEAD_DIM :],
-                )
-                roped = u_bank[:, :, : ROPE_HEADS * HEAD_DIM]
-                by_cos = rope_pool.tile([P, ROPE_HEADS, CHUNK_TILES, HEAD_DIM], F32)
-                nc.vector.tensor_tensor(
-                    out=by_cos[:],
-                    in0=roped.rearrange("p j (h d) -> p h j d", h=ROPE_HEADS),
-                    in1=cos_tab[:, j_batch : j_batch + CHUNK_TILES]
-                    .rearrange("p j i two -> p j (i two)")
-                    .unsqueeze(1)
-                    .to_broadcast([P, ROPE_HEADS, CHUNK_TILES, HEAD_DIM]),
-                    op=ALU.mult,
-                )
-                by_sin = rope_pool.tile([P, 2, ROPE_HEADS, CHUNK_TILES, PAIRS], F32)
-                halves = roped.rearrange("p j (h i two) -> p two h j i", h=ROPE_HEADS, two=2)
-                for two in range(2):
-                    nc.vector.tensor_tensor(
-                        out=by_sin[:, two],
-                        in0=halves[:, 1 - two],
-                        in1=sin_tab[:, two, j_batch : j_batch + CHUNK_TILES, :]
-                        .unsqueeze(1)
-                        .to_broadcast([P, ROPE_HEADS, CHUNK_TILES, PAIRS]),
-                        op=ALU.mult,
-                    )
-                nc.vector.tensor_tensor(
-                    out=out_sb[:, :ROPE_HEADS, j_store : j_store + CHUNK_TILES, :].rearrange(
-                        "p h j (i two) -> p h j i two", two=2
-                    ),
-                    in0=by_cos[:].rearrange("p h j (i two) -> p h j i two", two=2),
-                    in1=by_sin[:].rearrange("p two h j i -> p h j i two"),
-                    op=ALU.add,
-                )
-
-                if c % STORE_CHUNKS == STORE_CHUNKS - 1:
-                    j0 = j_batch + CHUNK_TILES - STORE_TILES
-                    nc.sync.dma_start(
-                        out=out_0[b, 0].rearrange("h (p j) d -> p h j d", j=TILES)[:, :, j0 : j0 + STORE_TILES, :],
-                        in_=out_sb[:, 0:2],
-                    )
-                    nc.sync.dma_start(
-                        out=out_1[b, 0].rearrange("(p j) d -> p j d", j=TILES)[:, j0 : j0 + STORE_TILES, :],
-                        in_=out_sb[:, 2],
-                    )
-                    nc.sync.dma_start(
-                        out=out_2[b, 0].rearrange("(p j) d -> p j d", j=TILES)[:, j0 : j0 + STORE_TILES, :],
-                        in_=out_sb[:, 3],
-                    )
+        for n in range(ALL_CHUNKS + 2):
+            if n + X_BUFS - 1 < ALL_CHUNKS:
+                load(n + X_BUFS - 1)
+            if n < ALL_CHUNKS:
+                transpose_and_quantise(n, 0)
+            if 0 <= n - 2:
+                rope_sum_and_store(n - 2)
+            if n < ALL_CHUNKS:
+                transpose_and_quantise(n, 1)
+            if 0 <= n - 1 < ALL_CHUNKS:
+                project(n - 1)
+                rope_products(n - 1)

@@ -35,7 +35,8 @@ QUANT_TILES = 2
 STORE_CHUNKS = 2
 STORE_TILES = STORE_CHUNKS * CHUNK_TILES
 ALL_CHUNKS = BATCH * CHUNKS
-X_BUFS = 8
+HALVES = CHUNK_TILES // QUANT_TILES
+STORES = ALL_CHUNKS // STORE_CHUNKS
 
 ROPE_THETA = 1e6
 YARN_FACTOR = 64.0
@@ -85,18 +86,16 @@ def build_rope_tables(nc, pool, cos_tab, sin_tab):
         op0=ALU.add,
         op1=ALU.subtract,
     )
-    near = pool.tile(both, F32)
-    nc.vector.tensor_tensor(out=near[:], in0=coarse[:], in1=whole[:], op=ALU.subtract)
     frac = pool.tile(both, F32)
+    nc.vector.tensor_tensor(out=frac[:], in0=coarse[:], in1=whole[:], op=ALU.subtract)
     nc.vector.tensor_tensor(
-        out=frac[:], in0=near[:], in1=fine[:].unsqueeze(1).to_broadcast(both), op=ALU.add
+        out=frac[:], in0=frac[:], in1=fine[:].unsqueeze(1).to_broadcast(both), op=ALU.add
     )
 
-    half_sin = pool.tile(both, F32)
-    nc.scalar.activation(out=half_sin[:], in_=frac[:], func=ACT.Sin, scale=math.pi)
     versine = pool.tile(both, F32)
+    nc.scalar.activation(out=versine[:], in_=frac[:], func=ACT.Sin, scale=math.pi)
     nc.scalar.activation(
-        out=versine[:], in_=half_sin[:], func=ACT.Square, scale=math.sqrt(2.0 * ATTN_FACTOR)
+        out=versine[:], in_=versine[:], func=ACT.Square, scale=math.sqrt(2.0 * ATTN_FACTOR)
     )
 
     nc.vector.tensor_scalar(
@@ -124,27 +123,27 @@ def tile_causalselfattentiongqa_pa_t_kernel(tc, x, w_qkv, out_0, out_1, out_2):
     nc = tc.nc
     with ExitStack() as ctx:
         const = ctx.enter_context(tc.tile_pool(name="const", bufs=1))
-        x_pool = ctx.enter_context(tc.tile_pool(name="x", bufs=X_BUFS))
+        x_pool = ctx.enter_context(tc.tile_pool(name="x", bufs=ALL_CHUNKS * HALVES))
         mx_pool = ctx.enter_context(tc.tile_pool(name="mx", bufs=3))
         rope_pool = ctx.enter_context(tc.tile_pool(name="rope", bufs=3))
-        out_pool = ctx.enter_context(tc.tile_pool(name="out", bufs=3))
+        out_pool = ctx.enter_context(tc.tile_pool(name="out", bufs=STORES))
         psum_t = ctx.enter_context(tc.psum_pool(name="psum_t", bufs=6))
         psum_u = ctx.enter_context(tc.psum_pool(name="psum_u", bufs=2))
         ctx.enter_context(tc.manual_schedule())
 
         x_rows = x.rearrange("b (p j) d -> b p (j d)", j=TILES)
-        x_chunks = {}
+        x_parts = {}
         mx_tiles = {}
         u_banks = {}
         rope_tiles = {}
         out_tiles = {}
 
-        def load(n):
+        def load(n, half):
             b, c = divmod(n, CHUNKS)
-            x_chunk = x_pool.tile([P, CHUNK_TILES * D_MODEL], BF16)
-            first = c * CHUNK_TILES * D_MODEL
-            nc.sync.dma_start(out=x_chunk[:], in_=x_rows[b, :, first : first + CHUNK_TILES * D_MODEL])
-            x_chunks[n] = x_chunk
+            x_part = x_pool.tile([P, QUANT_TILES * D_MODEL], BF16)
+            first = (c * CHUNK_TILES + half * QUANT_TILES) * D_MODEL
+            nc.sync.dma_start(out=x_part[:], in_=x_rows[b, :, first : first + QUANT_TILES * D_MODEL])
+            x_parts[(n, half)] = x_part
 
         def transpose_and_quantise(n, half):
             if half == 0:
@@ -153,17 +152,20 @@ def tile_causalselfattentiongqa_pa_t_kernel(tc, x, w_qkv, out_0, out_1, out_2):
                 scales = mx_pool.tile([P, CHUNK_TILES * PASSES * P], U8, align_bytes=64)
                 mx_tiles[n] = (grouped, codes, scales)
             grouped, codes, scales = mx_tiles[n]
-            x_words = x_chunks[n][:].bitcast(F32)
+            x_words = x_parts[(n, half)][:].bitcast(F32)
             grouped_words = grouped[:].bitcast(F32).rearrange(
                 "p (j g c u) -> p j g c u", j=CHUNK_TILES, g=PASSES, u=WORD_BLOCKS
             )
-            for jj in range(half * QUANT_TILES, (half + 1) * QUANT_TILES):
+            for jq in range(QUANT_TILES):
                 xt = psum_t.tile([P, PASSES, WORD_BLOCKS, P], F32)
                 for g in range(PASSES):
                     for u in range(WORD_BLOCKS):
-                        col = ((jj * PASSES + g) * WORD_BLOCKS + u) * P
+                        col = ((jq * PASSES + g) * WORD_BLOCKS + u) * P
                         nc.tensor.transpose(xt[:, g, u, :], x_words[:, col : col + P], identity[:])
-                nc.scalar.copy(out=grouped_words[:, jj], in_=xt[:].rearrange("p g u c -> p g c u"))
+                nc.scalar.copy(
+                    out=grouped_words[:, half * QUANT_TILES + jq],
+                    in_=xt[:].rearrange("p g u c -> p g c u"),
+                )
             words = QUANT_TILES * PASSES * P
             lo = half * words
             nc.vector.quantize_mx(
@@ -254,14 +256,16 @@ def tile_causalselfattentiongqa_pa_t_kernel(tc, x, w_qkv, out_0, out_1, out_2):
                     in_=out_sb[:, 3],
                 )
 
-        load(0)
+        for half in range(HALVES):
+            load(0, half)
         w_raw = const.tile([P, PASSES, PACK, FEATURES], BF16)
         nc.sync.dma_start(
             out=w_raw[:].rearrange("p g (u e) c -> p (g u) (e c)", e=2),
             in_=w_qkv.rearrange("(gu p e) c -> p gu (e c)", p=P, e=2),
         )
-        for n in range(1, X_BUFS - 1):
-            load(n)
+        for n in range(1, ALL_CHUNKS):
+            for half in range(HALVES):
+                load(n, half)
 
         cos_tab = const.tile([P, TILES, PAIRS, 2], F32)
         sin_tab = const.tile([P, 2, TILES, PAIRS], F32)
@@ -281,8 +285,6 @@ def tile_causalselfattentiongqa_pa_t_kernel(tc, x, w_qkv, out_0, out_1, out_2):
         )
 
         for n in range(ALL_CHUNKS + 2):
-            if n + X_BUFS - 1 < ALL_CHUNKS:
-                load(n + X_BUFS - 1)
             if n < ALL_CHUNKS:
                 transpose_and_quantise(n, 0)
             if 0 <= n - 2:

@@ -22,6 +22,7 @@ PAIRS = HEAD_DIM // 2
 ROPE_HEADS = 3
 HEADS = 4
 FEATURES = HEADS * HEAD_DIM
+ROPE_COLS = ROPE_HEADS * HEAD_DIM
 
 PACK = 4
 K_PASS = P * PACK
@@ -55,29 +56,25 @@ def turns_per_position(i):
     return (base * (1.0 - ramp) + (base / YARN_FACTOR) * ramp) / (2.0 * math.pi)
 
 
-def build_rope_tables(nc, pool, cos_tab, sin_tab):
-    both = [P, 2, TILES, PAIRS]
+def build_rope_versines(nc, pool):
     pos_int = pool.tile([P, TILES], I32)
     nc.gpsimd.iota(pos_int[:], pattern=[[1, TILES]], base=0, channel_multiplier=TILES)
     pos = pool.tile([P, TILES], F32)
     nc.vector.tensor_copy(out=pos[:], in_=pos_int[:])
+    sin_first = pool.tile([P, 1], F32)
+    nc.scalar.activation(out=sin_first[:], in_=pos[:, 0:1], func=ACT.Sin, scale=0.0)
 
-    coarse = pool.tile(both, F32)
-    fine = pool.tile([P, TILES, PAIRS], F32)
+    coarse = pool.tile([P, PAIRS, TILES], F32)
+    fine = pool.tile([P, PAIRS, TILES], F32)
     for i in range(PAIRS):
         turns = turns_per_position(i)
         turns_coarse = round(turns * TURN_GRID) / TURN_GRID
         nc.vector.tensor_scalar(
-            out=coarse[:, 0, :, i], in0=pos[:], scalar1=turns_coarse, scalar2=None, op0=ALU.mult
+            out=coarse[:, i, :], in0=pos[:], scalar1=turns_coarse, scalar2=None, op0=ALU.mult
         )
-        nc.vector.tensor_scalar(
-            out=fine[:, :, i], in0=pos[:], scalar1=turns - turns_coarse, scalar2=None, op0=ALU.mult
-        )
-    nc.vector.tensor_scalar(
-        out=coarse[:, 1], in0=coarse[:, 0], scalar1=-0.25, scalar2=None, op0=ALU.add
-    )
+        nc.scalar.mul(out=fine[:, i, :], in_=pos[:], mul=turns - turns_coarse)
 
-    whole = pool.tile(both, F32)
+    whole = pool.tile([P, PAIRS, TILES], F32)
     nc.vector.tensor_scalar(
         out=whole[:],
         in0=coarse[:],
@@ -86,36 +83,40 @@ def build_rope_tables(nc, pool, cos_tab, sin_tab):
         op0=ALU.add,
         op1=ALU.subtract,
     )
-    frac = pool.tile(both, F32)
-    nc.vector.tensor_tensor(out=frac[:], in0=coarse[:], in1=whole[:], op=ALU.subtract)
-    nc.vector.tensor_tensor(
-        out=frac[:], in0=frac[:], in1=fine[:].unsqueeze(1).to_broadcast(both), op=ALU.add
-    )
+    frac = pool.tile([P, 2, PAIRS, TILES], F32)
+    nc.vector.tensor_tensor(out=frac[:, 0], in0=coarse[:], in1=whole[:], op=ALU.subtract)
+    nc.vector.tensor_tensor(out=frac[:, 0], in0=frac[:, 0], in1=fine[:], op=ALU.add)
+    nc.vector.tensor_scalar(out=frac[:, 1], in0=frac[:, 0], scalar1=-0.25, scalar2=None, op0=ALU.add)
 
-    versine = pool.tile(both, F32)
+    versine = pool.tile([P, 2, PAIRS, TILES], F32)
     nc.scalar.activation(out=versine[:], in_=frac[:], func=ACT.Sin, scale=math.pi)
     nc.scalar.activation(
         out=versine[:], in_=versine[:], func=ACT.Square, scale=math.sqrt(2.0 * ATTN_FACTOR)
     )
+    return versine
 
+
+def finish_rope_table(nc, versine, rope_tab):
+    cos_versine = versine[:, 0].rearrange("p i j -> p j i")
+    sin_versine = versine[:, 1].rearrange("p i j -> p j i")
     nc.vector.tensor_scalar(
-        out=cos_tab[:],
-        in0=versine[:, 0].unsqueeze(3).to_broadcast([P, TILES, PAIRS, 2]),
+        out=rope_tab[:, 0],
+        in0=cos_versine.unsqueeze(3).to_broadcast([P, TILES, PAIRS, 2]),
         scalar1=-1.0,
         scalar2=ATTN_FACTOR,
         op0=ALU.mult,
         op1=ALU.add,
     )
     nc.vector.tensor_scalar(
-        out=sin_tab[:, 0], in0=versine[:, 1], scalar1=ATTN_FACTOR, scalar2=None, op0=ALU.subtract
-    )
-    nc.vector.tensor_scalar(
-        out=sin_tab[:, 1],
-        in0=versine[:, 1],
+        out=rope_tab[:, 1, :, :, 0],
+        in0=sin_versine,
         scalar1=-1.0,
         scalar2=ATTN_FACTOR,
         op0=ALU.mult,
         op1=ALU.add,
+    )
+    nc.vector.tensor_scalar(
+        out=rope_tab[:, 1, :, :, 1], in0=sin_versine, scalar1=ATTN_FACTOR, scalar2=None, op0=ALU.subtract
     )
 
 
@@ -202,43 +203,37 @@ def tile_causalselfattentiongqa_pa_t_kernel(tc, x, w_qkv, out_0, out_1, out_2):
             j_store = (c % STORE_CHUNKS) * CHUNK_TILES
             nc.scalar.copy(
                 out=out_sb[:, ROPE_HEADS, j_store : j_store + CHUNK_TILES, :],
-                in_=u_bank[:, :, ROPE_HEADS * HEAD_DIM :],
+                in_=u_bank[:, :, ROPE_COLS:],
             )
-            roped = u_bank[:, :, : ROPE_HEADS * HEAD_DIM]
-            by_cos = rope_pool.tile([P, ROPE_HEADS, CHUNK_TILES, HEAD_DIM], F32)
+            shape = [P, 2, CHUNK_TILES, HEAD_DIM, ROPE_HEADS]
+            prod = rope_pool.tile(shape, F32)
             nc.vector.tensor_tensor(
-                out=by_cos[:],
-                in0=roped.rearrange("p j (h d) -> p h j d", h=ROPE_HEADS),
-                in1=cos_tab[:, j_batch : j_batch + CHUNK_TILES]
-                .rearrange("p j i two -> p j (i two)")
+                out=prod[:],
+                in0=u_bank[:, :, :ROPE_COLS]
+                .rearrange("p j (d h) -> p j d h", h=ROPE_HEADS)
                 .unsqueeze(1)
-                .to_broadcast([P, ROPE_HEADS, CHUNK_TILES, HEAD_DIM]),
+                .to_broadcast(shape),
+                in1=rope_tab[:, :, j_batch : j_batch + CHUNK_TILES]
+                .rearrange("p r j i two -> p r j (i two)")
+                .unsqueeze(4)
+                .to_broadcast(shape),
                 op=ALU.mult,
             )
-            by_sin = rope_pool.tile([P, 2, ROPE_HEADS, CHUNK_TILES, PAIRS], F32)
-            halves = roped.rearrange("p j (h i two) -> p two h j i", h=ROPE_HEADS, two=2)
-            for two in range(2):
-                nc.vector.tensor_tensor(
-                    out=by_sin[:, two],
-                    in0=halves[:, 1 - two],
-                    in1=sin_tab[:, two, j_batch : j_batch + CHUNK_TILES, :]
-                    .unsqueeze(1)
-                    .to_broadcast([P, ROPE_HEADS, CHUNK_TILES, PAIRS]),
-                    op=ALU.mult,
-                )
-            rope_tiles[n] = (by_cos, by_sin)
+            rope_tiles[n] = prod
 
         def rope_sum_and_store(n):
             b, c = divmod(n, CHUNKS)
             out_sb = out_tiles[n // STORE_CHUNKS]
-            by_cos, by_sin = rope_tiles[n]
+            prod = rope_tiles[n]
             j_store = (c % STORE_CHUNKS) * CHUNK_TILES
+            by_cos = prod[:, 0].rearrange("p j (i two) h -> p h j i two", two=2)
+            by_sin = prod[:, 1].rearrange("p j (i two) h -> p h j i two", two=2)
             nc.vector.tensor_tensor(
                 out=out_sb[:, :ROPE_HEADS, j_store : j_store + CHUNK_TILES, :].rearrange(
                     "p h j (i two) -> p h j i two", two=2
                 ),
-                in0=by_cos[:].rearrange("p h j (i two) -> p h j i two", two=2),
-                in1=by_sin[:].rearrange("p two h j i -> p h j i two"),
+                in0=by_cos,
+                in1=by_sin[:, :, :, :, ::-1],
                 op=ALU.add,
             )
             if c % STORE_CHUNKS == STORE_CHUNKS - 1:
@@ -256,26 +251,29 @@ def tile_causalselfattentiongqa_pa_t_kernel(tc, x, w_qkv, out_0, out_1, out_2):
                     in_=out_sb[:, 3],
                 )
 
-        for half in range(HALVES):
-            load(0, half)
+        load(0, 0)
         w_raw = const.tile([P, PASSES, PACK, FEATURES], BF16)
         nc.sync.dma_start(
             out=w_raw[:].rearrange("p g (u e) c -> p (g u) (e c)", e=2),
             in_=w_qkv.rearrange("(gu p e) c -> p gu (e c)", p=P, e=2),
         )
-        for n in range(1, ALL_CHUNKS):
-            for half in range(HALVES):
-                load(n, half)
+        for part in range(1, ALL_CHUNKS * HALVES):
+            load(part // HALVES, part % HALVES)
 
-        cos_tab = const.tile([P, TILES, PAIRS, 2], F32)
-        sin_tab = const.tile([P, 2, TILES, PAIRS], F32)
-        build_rope_tables(nc, const, cos_tab, sin_tab)
+        versine = build_rope_versines(nc, const)
 
         identity = const.tile([P, P], F32)
         make_identity(nc, identity[:])
 
         w_grouped = const.tile([P, PASSES, FEATURES, PACK], BF16, align_bytes=64)
-        nc.vector.tensor_copy(out=w_grouped[:], in_=w_raw[:].rearrange("p g t c -> p g c t"))
+        nc.vector.tensor_copy(
+            out=w_grouped[:, :, :ROPE_COLS, :].rearrange("p g (d h) t -> p g d h t", h=ROPE_HEADS),
+            in_=w_raw[:, :, :, :ROPE_COLS].rearrange("p g t (h d) -> p g d h t", h=ROPE_HEADS),
+        )
+        nc.vector.tensor_copy(
+            out=w_grouped[:, :, ROPE_COLS:, :],
+            in_=w_raw[:, :, :, ROPE_COLS:].rearrange("p g t c -> p g c t"),
+        )
         w_codes = const.tile([P, PASSES * FEATURES], U32, align_bytes=64)
         w_scales = const.tile([P, PASSES * FEATURES], U8, align_bytes=64)
         nc.vector.quantize_mx(
@@ -284,6 +282,7 @@ def tile_causalselfattentiongqa_pa_t_kernel(tc, x, w_qkv, out_0, out_1, out_2):
             in_=w_grouped[:].rearrange("p g c t -> p (g c t)"),
         )
 
+        rope_tab = const.tile([P, 2, TILES, PAIRS, 2], F32)
         for n in range(ALL_CHUNKS + 2):
             if n < ALL_CHUNKS:
                 transpose_and_quantise(n, 0)
@@ -291,6 +290,8 @@ def tile_causalselfattentiongqa_pa_t_kernel(tc, x, w_qkv, out_0, out_1, out_2):
                 rope_sum_and_store(n - 2)
             if n < ALL_CHUNKS:
                 transpose_and_quantise(n, 1)
+            if n == 0:
+                finish_rope_table(nc, versine, rope_tab)
             if 0 <= n - 1 < ALL_CHUNKS:
                 project(n - 1)
                 rope_products(n - 1)

@@ -83,12 +83,13 @@ def build_rope_versines(nc, pool):
         op0=ALU.add,
         op1=ALU.subtract,
     )
-    frac = pool.tile([P, 2, PAIRS, TILES], F32)
+    frac = pool.tile([P, 3, PAIRS, TILES], F32)
     nc.vector.tensor_tensor(out=frac[:, 0], in0=coarse[:], in1=whole[:], op=ALU.subtract)
     nc.vector.tensor_tensor(out=frac[:, 0], in0=frac[:, 0], in1=fine[:], op=ALU.add)
-    nc.vector.tensor_scalar(out=frac[:, 1], in0=frac[:, 0], scalar1=-0.25, scalar2=None, op0=ALU.add)
+    nc.vector.tensor_scalar(out=frac[:, 1], in0=frac[:, 0], scalar1=0.25, scalar2=None, op0=ALU.add)
+    nc.vector.tensor_scalar(out=frac[:, 2], in0=frac[:, 0], scalar1=-0.25, scalar2=None, op0=ALU.add)
 
-    versine = pool.tile([P, 2, PAIRS, TILES], F32)
+    versine = pool.tile([P, 3, PAIRS, TILES], F32)
     nc.scalar.activation(out=versine[:], in_=frac[:], func=ACT.Sin, scale=math.pi)
     nc.scalar.activation(
         out=versine[:], in_=versine[:], func=ACT.Square, scale=math.sqrt(2.0 * ATTN_FACTOR)
@@ -96,27 +97,22 @@ def build_rope_versines(nc, pool):
     return versine
 
 
-def finish_rope_table(nc, versine, rope_tab):
-    cos_versine = versine[:, 0].rearrange("p i j -> p j i")
-    sin_versine = versine[:, 1].rearrange("p i j -> p j i")
+def finish_rope_tables(nc, versine, cos_tab, sin_tab):
     nc.vector.tensor_scalar(
-        out=rope_tab[:, 0],
-        in0=cos_versine.unsqueeze(3).to_broadcast([P, TILES, PAIRS, 2]),
+        out=cos_tab[:],
+        in0=versine[:, 0].rearrange("p i j -> p j i").unsqueeze(3).to_broadcast([P, TILES, PAIRS, 2]),
         scalar1=-1.0,
         scalar2=ATTN_FACTOR,
         op0=ALU.mult,
         op1=ALU.add,
     )
     nc.vector.tensor_scalar(
-        out=rope_tab[:, 1, :, :, 0],
-        in0=sin_versine,
+        out=sin_tab[:],
+        in0=versine[:, 1:3].rearrange("p s i j -> p j i s"),
         scalar1=-1.0,
         scalar2=ATTN_FACTOR,
         op0=ALU.mult,
         op1=ALU.add,
-    )
-    nc.vector.tensor_scalar(
-        out=rope_tab[:, 1, :, :, 1], in0=sin_versine, scalar1=ATTN_FACTOR, scalar2=None, op0=ALU.subtract
     )
 
 
@@ -124,7 +120,7 @@ def tile_causalselfattentiongqa_pa_t_kernel(tc, x, w_qkv, out_0, out_1, out_2):
     nc = tc.nc
     with ExitStack() as ctx:
         const = ctx.enter_context(tc.tile_pool(name="const", bufs=1))
-        x_pool = ctx.enter_context(tc.tile_pool(name="x", bufs=ALL_CHUNKS * HALVES))
+        x_pool = ctx.enter_context(tc.tile_pool(name="x", bufs=ALL_CHUNKS))
         mx_pool = ctx.enter_context(tc.tile_pool(name="mx", bufs=3))
         rope_pool = ctx.enter_context(tc.tile_pool(name="rope", bufs=3))
         out_pool = ctx.enter_context(tc.tile_pool(name="out", bufs=STORES))
@@ -133,18 +129,21 @@ def tile_causalselfattentiongqa_pa_t_kernel(tc, x, w_qkv, out_0, out_1, out_2):
         ctx.enter_context(tc.manual_schedule())
 
         x_rows = x.rearrange("b (p j) d -> b p (j d)", j=TILES)
-        x_parts = {}
+        x_chunks = {}
         mx_tiles = {}
         u_banks = {}
         rope_tiles = {}
         out_tiles = {}
 
-        def load(n, half):
+        def load(n, parts):
             b, c = divmod(n, CHUNKS)
-            x_part = x_pool.tile([P, QUANT_TILES * D_MODEL], BF16)
-            first = (c * CHUNK_TILES + half * QUANT_TILES) * D_MODEL
-            nc.sync.dma_start(out=x_part[:], in_=x_rows[b, :, first : first + QUANT_TILES * D_MODEL])
-            x_parts[(n, half)] = x_part
+            x_chunk = x_pool.tile([P, CHUNK_TILES * D_MODEL], BF16)
+            width = CHUNK_TILES * D_MODEL // parts
+            for part in range(parts):
+                lo = part * width
+                first = c * CHUNK_TILES * D_MODEL + lo
+                nc.sync.dma_start(out=x_chunk[:, lo : lo + width], in_=x_rows[b, :, first : first + width])
+            x_chunks[n] = x_chunk
 
         def transpose_and_quantise(n, half):
             if half == 0:
@@ -153,20 +152,17 @@ def tile_causalselfattentiongqa_pa_t_kernel(tc, x, w_qkv, out_0, out_1, out_2):
                 scales = mx_pool.tile([P, CHUNK_TILES * PASSES * P], U8, align_bytes=64)
                 mx_tiles[n] = (grouped, codes, scales)
             grouped, codes, scales = mx_tiles[n]
-            x_words = x_parts[(n, half)][:].bitcast(F32)
+            x_words = x_chunks[n][:].bitcast(F32)
             grouped_words = grouped[:].bitcast(F32).rearrange(
                 "p (j g c u) -> p j g c u", j=CHUNK_TILES, g=PASSES, u=WORD_BLOCKS
             )
-            for jq in range(QUANT_TILES):
+            for jj in range(half * QUANT_TILES, (half + 1) * QUANT_TILES):
                 xt = psum_t.tile([P, PASSES, WORD_BLOCKS, P], F32)
                 for g in range(PASSES):
                     for u in range(WORD_BLOCKS):
-                        col = ((jq * PASSES + g) * WORD_BLOCKS + u) * P
+                        col = ((jj * PASSES + g) * WORD_BLOCKS + u) * P
                         nc.tensor.transpose(xt[:, g, u, :], x_words[:, col : col + P], identity[:])
-                nc.scalar.copy(
-                    out=grouped_words[:, half * QUANT_TILES + jq],
-                    in_=xt[:].rearrange("p g u c -> p g c u"),
-                )
+                nc.scalar.copy(out=grouped_words[:, jj], in_=xt[:].rearrange("p g u c -> p g c u"))
             words = QUANT_TILES * PASSES * P
             lo = half * words
             nc.vector.quantize_mx(
@@ -205,35 +201,37 @@ def tile_causalselfattentiongqa_pa_t_kernel(tc, x, w_qkv, out_0, out_1, out_2):
                 out=out_sb[:, ROPE_HEADS, j_store : j_store + CHUNK_TILES, :],
                 in_=u_bank[:, :, ROPE_COLS:],
             )
-            shape = [P, 2, CHUNK_TILES, HEAD_DIM, ROPE_HEADS]
-            prod = rope_pool.tile(shape, F32)
+            roped = u_bank[:, :, :ROPE_COLS]
+            by_cos = rope_pool.tile([P, CHUNK_TILES, ROPE_HEADS, HEAD_DIM], F32)
             nc.vector.tensor_tensor(
-                out=prod[:],
-                in0=u_bank[:, :, :ROPE_COLS]
-                .rearrange("p j (d h) -> p j d h", h=ROPE_HEADS)
-                .unsqueeze(1)
-                .to_broadcast(shape),
-                in1=rope_tab[:, :, j_batch : j_batch + CHUNK_TILES]
-                .rearrange("p r j i two -> p r j (i two)")
-                .unsqueeze(4)
-                .to_broadcast(shape),
+                out=by_cos[:],
+                in0=roped.rearrange("p j (h d) -> p j h d", h=ROPE_HEADS),
+                in1=cos_tab[:, j_batch : j_batch + CHUNK_TILES]
+                .rearrange("p j i two -> p j (i two)")
+                .unsqueeze(2)
+                .to_broadcast([P, CHUNK_TILES, ROPE_HEADS, HEAD_DIM]),
                 op=ALU.mult,
             )
-            rope_tiles[n] = prod
+            by_sin = rope_pool.tile([P, CHUNK_TILES, ROPE_HEADS, PAIRS, 2], F32)
+            nc.vector.tensor_tensor(
+                out=by_sin[:],
+                in0=roped.rearrange("p j (h i two) -> p j h i two", h=ROPE_HEADS, two=2)[:, :, :, :, ::-1],
+                in1=sin_tab[:, j_batch : j_batch + CHUNK_TILES]
+                .unsqueeze(2)
+                .to_broadcast([P, CHUNK_TILES, ROPE_HEADS, PAIRS, 2]),
+                op=ALU.mult,
+            )
+            rope_tiles[n] = (by_cos, by_sin)
 
         def rope_sum_and_store(n):
             b, c = divmod(n, CHUNKS)
             out_sb = out_tiles[n // STORE_CHUNKS]
-            prod = rope_tiles[n]
+            by_cos, by_sin = rope_tiles[n]
             j_store = (c % STORE_CHUNKS) * CHUNK_TILES
-            by_cos = prod[:, 0].rearrange("p j (i two) h -> p h j i two", two=2)
-            by_sin = prod[:, 1].rearrange("p j (i two) h -> p h j i two", two=2)
             nc.vector.tensor_tensor(
-                out=out_sb[:, :ROPE_HEADS, j_store : j_store + CHUNK_TILES, :].rearrange(
-                    "p h j (i two) -> p h j i two", two=2
-                ),
-                in0=by_cos,
-                in1=by_sin[:, :, :, :, ::-1],
+                out=out_sb[:, :ROPE_HEADS, j_store : j_store + CHUNK_TILES, :].rearrange("p h j d -> p j h d"),
+                in0=by_cos[:],
+                in1=by_sin[:].rearrange("p j h i two -> p j h (i two)"),
                 op=ALU.add,
             )
             if c % STORE_CHUNKS == STORE_CHUNKS - 1:
@@ -251,14 +249,14 @@ def tile_causalselfattentiongqa_pa_t_kernel(tc, x, w_qkv, out_0, out_1, out_2):
                     in_=out_sb[:, 3],
                 )
 
-        load(0, 0)
+        load(0, HALVES)
         w_raw = const.tile([P, PASSES, PACK, FEATURES], BF16)
         nc.sync.dma_start(
             out=w_raw[:].rearrange("p g (u e) c -> p (g u) (e c)", e=2),
             in_=w_qkv.rearrange("(gu p e) c -> p gu (e c)", p=P, e=2),
         )
-        for part in range(1, ALL_CHUNKS * HALVES):
-            load(part // HALVES, part % HALVES)
+        for n in range(1, ALL_CHUNKS):
+            load(n, 1)
 
         versine = build_rope_versines(nc, const)
 
@@ -266,14 +264,7 @@ def tile_causalselfattentiongqa_pa_t_kernel(tc, x, w_qkv, out_0, out_1, out_2):
         make_identity(nc, identity[:])
 
         w_grouped = const.tile([P, PASSES, FEATURES, PACK], BF16, align_bytes=64)
-        nc.vector.tensor_copy(
-            out=w_grouped[:, :, :ROPE_COLS, :].rearrange("p g (d h) t -> p g d h t", h=ROPE_HEADS),
-            in_=w_raw[:, :, :, :ROPE_COLS].rearrange("p g t (h d) -> p g d h t", h=ROPE_HEADS),
-        )
-        nc.vector.tensor_copy(
-            out=w_grouped[:, :, ROPE_COLS:, :],
-            in_=w_raw[:, :, :, ROPE_COLS:].rearrange("p g t c -> p g c t"),
-        )
+        nc.vector.tensor_copy(out=w_grouped[:], in_=w_raw[:].rearrange("p g t c -> p g c t"))
         w_codes = const.tile([P, PASSES * FEATURES], U32, align_bytes=64)
         w_scales = const.tile([P, PASSES * FEATURES], U8, align_bytes=64)
         nc.vector.quantize_mx(
@@ -282,7 +273,10 @@ def tile_causalselfattentiongqa_pa_t_kernel(tc, x, w_qkv, out_0, out_1, out_2):
             in_=w_grouped[:].rearrange("p g c t -> p (g c t)"),
         )
 
-        rope_tab = const.tile([P, 2, TILES, PAIRS, 2], F32)
+        cos_tab = const.tile([P, TILES, PAIRS, 2], F32)
+        sin_tab = const.tile([P, TILES, PAIRS, 2], F32)
+        finish_rope_tables(nc, versine, cos_tab, sin_tab)
+
         for n in range(ALL_CHUNKS + 2):
             if n < ALL_CHUNKS:
                 transpose_and_quantise(n, 0)
@@ -290,8 +284,6 @@ def tile_causalselfattentiongqa_pa_t_kernel(tc, x, w_qkv, out_0, out_1, out_2):
                 rope_sum_and_store(n - 2)
             if n < ALL_CHUNKS:
                 transpose_and_quantise(n, 1)
-            if n == 0:
-                finish_rope_table(nc, versine, rope_tab)
             if 0 <= n - 1 < ALL_CHUNKS:
                 project(n - 1)
                 rope_products(n - 1)

import math
from contextlib import ExitStack

import concourse.mybir as mybir
from concourse.masks import make_identity

F32 = mybir.dt.float32
BF16 = mybir.dt.bfloat16
I32 = mybir.dt.int32
U32 = mybir.dt.uint32
U8 = mybir.dt.uint8
FP8X4 = mybir.dt.float8_e4m3fn_x4
ALU = mybir.AluOpType
ACT = mybir.ActivationFunctionType

P = 128
BATCH = 4
SEQ = 2048
D_MODEL = 1024
HEAD_DIM = 32
PAIRS = HEAD_DIM // 2
ROPE_HEADS = 3
HEADS = 4
FEATURES = HEADS * HEAD_DIM
ROPE_COLS = ROPE_HEADS * HEAD_DIM

PACK = 4
K_PASS = P * PACK
PASSES = D_MODEL // K_PASS
WORD_BLOCKS = 2

TILES = SEQ // P
CHUNK_TILES = 4
CHUNKS = TILES // CHUNK_TILES
QUANT_TILES = 2
STORE_CHUNKS = 2
STORE_TILES = STORE_CHUNKS * CHUNK_TILES
ALL_CHUNKS = BATCH * CHUNKS
HALVES = CHUNK_TILES // QUANT_TILES
STORES = ALL_CHUNKS // STORE_CHUNKS

ROPE_THETA = 1e6
YARN_FACTOR = 64.0
RAMP_LOW = 5.0
RAMP_HIGH = 8.0
ATTN_FACTOR = 0.1 * math.log(YARN_FACTOR) + 1.0
TURN_GRID = 2.0**15
ROUND_MAGIC = 1.5 * 2.0**23

FLOPS = 2 * BATCH * SEQ * D_MODEL * FEATURES


def turns_per_position(i):
    base = ROPE_THETA ** (-i / PAIRS)
    ramp = min(max((i - RAMP_LOW) / (RAMP_HIGH - RAMP_LOW), 0.0), 1.0)
    return (base * (1.0 - ramp) + (base / YARN_FACTOR) * ramp) / (2.0 * math.pi)


def build_rope_versines(nc, pool):
    pos_int = pool.tile([P, TILES], I32)
    nc.gpsimd.iota(pos_int[:], pattern=[[1, TILES]], base=0, channel_multiplier=TILES)
    pos = pool.tile([P, TILES], F32)
    nc.vector.tensor_copy(out=pos[:], in_=pos_int[:])
    sin_first = pool.tile([P, 1], F32)
    nc.scalar.activation(out=sin_first[:], in_=pos[:, 0:1], func=ACT.Sin, scale=0.0)

    coarse = pool.tile([P, PAIRS, TILES], F32)
    fine = pool.tile([P, PAIRS, TILES], F32)
    for i in range(PAIRS):
        turns = turns_per_position(i)
        turns_coarse = round(turns * TURN_GRID) / TURN_GRID
        nc.vector.tensor_scalar(
            out=coarse[:, i, :], in0=pos[:], scalar1=turns_coarse, scalar2=None, op0=ALU.mult
        )
        nc.scalar.mul(out=fine[:, i, :], in_=pos[:], mul=turns - turns_coarse)

    whole = pool.tile([P, PAIRS, TILES], F32)
    nc.vector.tensor_scalar(
        out=whole[:],
        in0=coarse[:],
        scalar1=ROUND_MAGIC,
        scalar2=ROUND_MAGIC,
        op0=ALU.add,
        op1=ALU.subtract,
    )
    frac = pool.tile([P, 3, PAIRS, TILES], F32)
    nc.vector.tensor_tensor(out=frac[:, 0], in0=coarse[:], in1=whole[:], op=ALU.subtract)
    nc.vector.tensor_tensor(out=frac[:, 0], in0=frac[:, 0], in1=fine[:], op=ALU.add)
    nc.vector.tensor_scalar(out=frac[:, 1], in0=frac[:, 0], scalar1=0.25, scalar2=None, op0=ALU.add)
    nc.vector.tensor_scalar(out=frac[:, 2], in0=frac[:, 0], scalar1=-0.25, scalar2=None, op0=ALU.add)

    versine = pool.tile([P, 3, PAIRS, TILES], F32)
    nc.scalar.activation(out=versine[:], in_=frac[:], func=ACT.Sin, scale=math.pi)
    nc.scalar.activation(
        out=versine[:], in_=versine[:], func=ACT.Square, scale=math.sqrt(2.0 * ATTN_FACTOR)
    )
    return versine


def finish_rope_tables(nc, versine, cos_tab, sin_tab):
    nc.vector.tensor_scalar(
        out=cos_tab[:],
        in0=versine[:, 0].rearrange("p i j -> p j i").unsqueeze(3).to_broadcast([P, TILES, PAIRS, 2]),
        scalar1=-1.0,
        scalar2=ATTN_FACTOR,
        op0=ALU.mult,
        op1=ALU.add,
    )
    nc.vector.tensor_scalar(
        out=sin_tab[:],
        in0=versine[:, 1:3].rearrange("p s i j -> p j i s"),
        scalar1=-1.0,
        scalar2=ATTN_FACTOR,
        op0=ALU.mult,
        op1=ALU.add,
    )


def tile_causalselfattentiongqa_pa_t_kernel(tc, x, w_qkv, out_0, out_1, out_2):
    nc = tc.nc
    with ExitStack() as ctx:
        const = ctx.enter_context(tc.tile_pool(name="const", bufs=1))
        x_pool = ctx.enter_context(tc.tile_pool(name="x", bufs=ALL_CHUNKS))
        mx_pool = ctx.enter_context(tc.tile_pool(name="mx", bufs=3))
        rope_pool = ctx.enter_context(tc.tile_pool(name="rope", bufs=3))
        out_pool = ctx.enter_context(tc.tile_pool(name="out", bufs=STORES))
        psum_t = ctx.enter_context(tc.psum_pool(name="psum_t", bufs=6))
        psum_u = ctx.enter_context(tc.psum_pool(name="psum_u", bufs=2))
        ctx.enter_context(tc.manual_schedule())

        x_rows = x.rearrange("b (p j) d -> b p (j d)", j=TILES)
        x_chunks = {}
        mx_tiles = {}
        u_banks = {}
        rope_tiles = {}
        out_tiles = {}

        def load(n, parts):
            b, c = divmod(n, CHUNKS)
            x_chunk = x_pool.tile([P, CHUNK_TILES * D_MODEL], BF16)
            width = CHUNK_TILES * D_MODEL // parts
            for part in range(parts):
                lo = part * width
                first = c * CHUNK_TILES * D_MODEL + lo
                nc.sync.dma_start(out=x_chunk[:, lo : lo + width], in_=x_rows[b, :, first : first + width])
            x_chunks[n] = x_chunk

        def transpose_and_quantise(n, half):
            if half == 0:
                grouped = mx_pool.tile([P, CHUNK_TILES * PASSES * P * PACK], BF16, align_bytes=64)
                codes = mx_pool.tile([P, CHUNK_TILES * PASSES * P], U32, align_bytes=64)
                scales = mx_pool.tile([P, CHUNK_TILES * PASSES * P], U8, align_bytes=64)
                mx_tiles[n] = (grouped, codes, scales)
            grouped, codes, scales = mx_tiles[n]
            x_words = x_chunks[n][:].bitcast(F32)
            grouped_words = grouped[:].bitcast(F32).rearrange(
                "p (j g c u) -> p j g c u", j=CHUNK_TILES, g=PASSES, u=WORD_BLOCKS
            )
            for jj in range(half * QUANT_TILES, (half + 1) * QUANT_TILES):
                xt = psum_t.tile([P, PASSES, WORD_BLOCKS, P], F32)
                for g in range(PASSES):
                    for u in range(WORD_BLOCKS):
                        col = ((jj * PASSES + g) * WORD_BLOCKS + u) * P
                        nc.tensor.transpose(xt[:, g, u, :], x_words[:, col : col + P], identity[:])
                nc.scalar.copy(out=grouped_words[:, jj], in_=xt[:].rearrange("p g u c -> p g c u"))
            words = QUANT_TILES * PASSES * P
            lo = half * words
            nc.vector.quantize_mx(
                out=codes[:, lo : lo + words].bitcast(FP8X4),
                scales=scales[:, lo : lo + words],
                in_=grouped[:, lo * PACK : (lo + words) * PACK],
            )

        def project(n):
            grouped, codes, scales = mx_tiles[n]
            u_bank = psum_u.tile([P, CHUNK_TILES, FEATURES], F32)
            for jj in range(CHUNK_TILES):
                for g in range(PASSES):
                    lo = (jj * PASSES + g) * P
                    nc.tensor.matmul_mx(
                        out=u_bank[:, jj, :],
                        lhsT=codes[:, lo : lo + P].bitcast(FP8X4),
                        lhsT_scale=scales[:, lo : lo + P],
                        rhs=w_codes[:, g * FEATURES : (g + 1) * FEATURES].bitcast(FP8X4),
                        rhs_scale=w_scales[:, g * FEATURES : (g + 1) * FEATURES],
                        start=(g == 0),
                        stop=(g == PASSES - 1),
                    )
            u_banks[n] = u_bank

        def rope_products(n):
            c = n % CHUNKS
            if c % STORE_CHUNKS == 0:
                out_sb = out_pool.tile([P, HEADS, STORE_TILES, HEAD_DIM], F32)
                out_tiles[n // STORE_CHUNKS] = out_sb
            out_sb = out_tiles[n // STORE_CHUNKS]
            u_bank = u_banks[n]
            j_batch = c * CHUNK_TILES
            j_store = (c % STORE_CHUNKS) * CHUNK_TILES
            nc.scalar.copy(
                out=out_sb[:, ROPE_HEADS, j_store : j_store + CHUNK_TILES, :],
                in_=u_bank[:, :, ROPE_COLS:],
            )
            roped = u_bank[:, :, :ROPE_COLS]
            by_cos = rope_pool.tile([P, CHUNK_TILES, ROPE_HEADS, HEAD_DIM], F32)
            nc.vector.tensor_tensor(
                out=by_cos[:],
                in0=roped.rearrange("p j (h d) -> p j h d", h=ROPE_HEADS),
                in1=cos_tab[:, j_batch : j_batch + CHUNK_TILES]
                .rearrange("p j i two -> p j (i two)")
                .unsqueeze(2)
                .to_broadcast([P, CHUNK_TILES, ROPE_HEADS, HEAD_DIM]),
                op=ALU.mult,
            )
            by_sin = rope_pool.tile([P, CHUNK_TILES, ROPE_HEADS, PAIRS, 2], F32)
            nc.vector.tensor_tensor(
                out=by_sin[:],
                in0=roped.rearrange("p j (h i two) -> p j h i two", h=ROPE_HEADS, two=2)[:, :, :, :, ::-1],
                in1=sin_tab[:, j_batch : j_batch + CHUNK_TILES]
                .unsqueeze(2)
                .to_broadcast([P, CHUNK_TILES, ROPE_HEADS, PAIRS, 2]),
                op=ALU.mult,
            )
            rope_tiles[n] = (by_cos, by_sin)

        def rope_sum_and_store(n):
            b, c = divmod(n, CHUNKS)
            out_sb = out_tiles[n // STORE_CHUNKS]
            by_cos, by_sin = rope_tiles[n]
            j_store = (c % STORE_CHUNKS) * CHUNK_TILES
            nc.vector.tensor_tensor(
                out=out_sb[:, :ROPE_HEADS, j_store : j_store + CHUNK_TILES, :].rearrange("p h j d -> p j h d"),
                in0=by_cos[:],
                in1=by_sin[:].rearrange("p j h i two -> p j h (i two)"),
                op=ALU.add,
            )
            if c % STORE_CHUNKS == STORE_CHUNKS - 1:
                j0 = (c + 1) * CHUNK_TILES - STORE_TILES
                nc.sync.dma_start(
                    out=out_0[b, 0].rearrange("h (p j) d -> p h j d", j=TILES)[:, :, j0 : j0 + STORE_TILES, :],
                    in_=out_sb[:, 0:2],
                )
                nc.sync.dma_start(
                    out=out_1[b, 0].rearrange("(p j) d -> p j d", j=TILES)[:, j0 : j0 + STORE_TILES, :],
                    in_=out_sb[:, 2],
                )
                nc.sync.dma_start(
                    out=out_2[b, 0].rearrange("(p j) d -> p j d", j=TILES)[:, j0 : j0 + STORE_TILES, :],
                    in_=out_sb[:, 3],
                )

        load(0, HALVES)
        w_raw = const.tile([P, PASSES, PACK, FEATURES], BF16)
        nc.sync.dma_start(
            out=w_raw[:].rearrange("p g (u e) c -> p (g u) (e c)", e=2),
            in_=w_qkv.rearrange("(gu p e) c -> p gu (e c)", p=P, e=2),
        )
        for n in range(1, ALL_CHUNKS):
            load(n, 1)

        versine = build_rope_versines(nc, const)

        identity = const.tile([P, P], F32)
        make_identity(nc, identity[:])

        w_grouped = const.tile([P, PASSES, FEATURES, PACK], BF16, align_bytes=64)
        nc.vector.tensor_copy(out=w_grouped[:], in_=w_raw[:].rearrange("p g t c -> p g c t"))
        w_codes = const.tile([P, PASSES * FEATURES], U32, align_bytes=64)
        w_scales = const.tile([P, PASSES * FEATURES], U8, align_bytes=64)
        nc.vector.quantize_mx(
            out=w_codes[:].bitcast(FP8X4),
            scales=w_scales[:],
            in_=w_grouped[:].rearrange("p g c t -> p (g c t)"),
        )

        cos_tab = const.tile([P, TILES, PAIRS, 2], F32)
        sin_tab = const.tile([P, TILES, PAIRS, 2], F32)
        finish_rope_tables(nc, versine, cos_tab, sin_tab)

        for n in range(ALL_CHUNKS + 2):
            if n < ALL_CHUNKS:
                transpose_and_quantise(n, 0)
            if 0 <= n - 2:
                rope_sum_and_store(n - 2)
            if n < ALL_CHUNKS:
                transpose_and_quantise(n, 1)
            if 0 <= n - 1 < ALL_CHUNKS:
                project(n - 1)
                rope_products(n - 1)
